import numpy as np
import ml_dtypes


def mxq(x, axis, fmt="e4m3"):
    dtype, down = {"e4m3": (ml_dtypes.float8_e4m3fn, 7), "e5m2": (ml_dtypes.float8_e5m2, 14)}[fmt]
    v = np.moveaxis(np.asarray(x, np.float32).astype(ml_dtypes.bfloat16).astype(np.float64), axis, -1)
    blocks = v.reshape(v.shape[:-1] + (-1, 32))
    amax = np.abs(blocks).max(-1, keepdims=True)
    byte = np.maximum(np.where(amax > 0, np.frexp(amax)[1] - 1 + 127, 0) - down, 1)
    scale = np.exp2(byte - 127.0)
    codes = (blocks / scale).astype(np.float32).astype(dtype).astype(np.float64)
    return np.moveaxis((codes * scale).reshape(v.shape), -1, axis)


WIDE = False


def mx_kscale(k):
    if not WIDE:
        return np.ones(k)
    levels = np.array([20, -20, 10, -10, 0])
    a = np.random.permutation(np.resize(levels, k // 512 * 4)).reshape(k // 512, 4)
    idx = np.arange(k)
    return np.exp2(a[idx // 512, idx % 128 // 32])


BF16 = ml_dtypes.bfloat16


def bf(x):
    return np.asarray(x, np.float32).astype(BF16)


def f64(x):
    return np.asarray(x).astype(np.float64)


BATCH, SIZE_IN, SIZE_OUT, STEPS = 4096, 1024, 512, 8


def _build_mask(size_in, size_out, steps):
    inp_el_counts = size_in // steps
    rows = np.arange(size_out)
    count = rows % inp_el_counts
    cols = np.arange(steps)[None, :] * inp_el_counts + count[:, None]
    mask = np.zeros((size_out, size_in))
    mask[rows[:, None], cols] = 1.0
    return mask


def setup_inputs():
    u = mx_kscale(SIZE_OUT)
    bound = np.sqrt(3.0 / STEPS)
    x = np.random.standard_normal((BATCH, SIZE_IN))
    weights = np.random.uniform(-bound, bound, (SIZE_OUT, SIZE_IN)) / u[:, None]
    bias = np.random.uniform(-0.5, 0.5, SIZE_OUT)
    mask = _build_mask(SIZE_IN, SIZE_OUT, STEPS)
    g = np.random.standard_normal((BATCH, SIZE_OUT)) * np.exp2(np.random.randint(-12, 1, (BATCH, 1))) * 8.0 * u[None, :]
    return {"x": bf(x), "weights": bf(weights), "bias": bf(bias), "mask": bf(mask), "grad_out": bf(g)}


def reference(x, weights, bias, mask, grad_out):
    w = f64(weights) * f64(mask)
    return mxq(f64(grad_out), 1, "e5m2") @ mxq(w, 0, "e4m3")

@@ -1,0 +1,138 @@
+from contextlib import ExitStack
+
+import concourse.mybir as mybir
+from concourse.masks import make_identity
+
+FLOPS = 2 * 4096 * 512 * 1024
+BYTES = 4096 * 1024 * 4 + 4096 * 512 * 2 + 2 * 512 * 1024 * 2
+
+F32 = mybir.dt.float32
+BF16 = mybir.dt.bfloat16
+U32 = mybir.dt.uint32
+U8 = mybir.dt.uint8
+E4M3X4 = mybir.dt.float8_e4m3fn_x4
+E5M2X4 = mybir.dt.float8_e5m2_x4
+
+P = 128
+K = 512
+N = 1024
+N_HALF = 512
+TILES = 32
+GROUP = 4
+GROUPS = TILES // GROUP
+LOAD_CHUNKS = (4, 4, 8, 16)
+VECTOR_BANKS = (2, 6)
+
+
+def tile_sparselayer_t_kernel(tc, x, weights, bias, mask, grad_out, out):
+    nc = tc.nc
+    with ExitStack() as ctx:
+        keep = ctx.enter_context(tc.tile_pool(name="keep", bufs=1))
+        stage = ctx.enter_context(tc.tile_pool(name="stage", bufs=3))
+        outs = ctx.enter_context(tc.tile_pool(name="outs", bufs=GROUPS))
+        tpsum = ctx.enter_context(tc.psum_pool(name="tpsum", bufs=2))
+        opsum = ctx.enter_context(tc.psum_pool(name="opsum", bufs=6))
+
+        w_raw = keep.tile([P, 4 * N], BF16)
+        m_raw = keep.tile([P, 4 * N], BF16)
+        nc.sync.dma_start(out=w_raw[:], in_=weights.rearrange("(p t) n -> p (t n)", t=4))
+        nc.sync.dma_start(out=m_raw[:], in_=mask.rearrange("(p t) n -> p (t n)", t=4))
+        g_rows = grad_out.rearrange("(p i) k -> p (i k)", i=TILES)
+        g_words = []
+        first = 0
+        for c, count in enumerate(LOAD_CHUNKS):
+            g_raw = keep.tile([P, count * K], BF16, name="g_raw%d" % c)
+            nc.sync.dma_start(out=g_raw[:], in_=g_rows[:, first * K : (first + count) * K])
+            g32 = g_raw[:].bitcast(F32)
+            for i in range(count):
+                g_words.append(g32[:, i * (K // 2) : (i + 1) * (K // 2)])
+            first += count
+
+        ident = keep.tile([P, P], F32)
+        make_identity(nc, ident[:])
+
+        w_grouped = keep.tile([P, 4 * N], BF16, align_bytes=64)
+        w_codes = keep.tile([P, N], U32, align_bytes=64)
+        w_scales = keep.tile([P, N], U8, align_bytes=64)
+
+        def prepare_w(h):
+            cols = slice(h * N_HALF, (h + 1) * N_HALF)
+            flat = slice(h * 4 * N_HALF, (h + 1) * 4 * N_HALF)
+            nc.vector.tensor_tensor(
+                out=w_grouped[:, flat].rearrange("p (n t) -> p n t", t=4),
+                in0=w_raw[:].rearrange("p (t n) -> p t n", t=4)[:, :, cols].rearrange("p t n -> p n t"),
+                in1=m_raw[:].rearrange("p (t n) -> p t n", t=4)[:, :, cols].rearrange("p t n -> p n t"),
+                op=mybir.AluOpType.mult,
+            )
+            nc.vector.quantize_mx(
+                out=w_codes[:, cols].bitcast(E4M3X4),
+                scales=w_scales[:, cols],
+                in_=w_grouped[:, flat],
+            )
+
+        def transpose_group(j, on_scalar):
+            g_grouped = stage.tile([P, GROUP * P * 4], BF16, align_bytes=64)
+            g_grouped32 = g_grouped[:].bitcast(F32)
+            for bank in range(GROUP // 2):
+                xt = tpsum.tile([P, 2, 2, P], F32)
+                for b in range(2):
+                    words = g_words[j * GROUP + 2 * bank + b].rearrange("p (w u) -> p u w", u=2)
+                    for u in range(2):
+                        nc.tensor.transpose(xt[:, b, u, :], words[:, u, :], ident[:])
+                dst = g_grouped32[:, bank * 512 : (bank + 1) * 512].rearrange(
+                    "p (b r u) -> p b r u", b=2, u=2
+                )
+                src = xt[:].rearrange("p b u r -> p b r u")
+                if on_scalar:
+                    nc.scalar.copy(out=dst, in_=src)
+                else:
+                    nc.vector.tensor_copy(out=dst, in_=src)
+            return g_grouped
+
+        def quantise_group(g_grouped):
+            g_codes = stage.tile([P, GROUP * P], U32, align_bytes=64)
+            g_scales = stage.tile([P, GROUP * P], U8, align_bytes=64)
+            nc.vector.quantize_mx(out=g_codes[:].bitcast(E5M2X4), scales=g_scales[:], in_=g_grouped[:])
+            return g_codes, g_scales
+
+        out_rows = out.rearrange("(p i) n -> p (i n)", i=TILES)
+
+        def multiply_group(j, g_codes, g_scales, pieces):
+            o_sb = outs.tile([P, GROUP * N], F32)
+            for b in range(GROUP):
+                rows = slice(b * P, (b + 1) * P)
+                for h in range(2):
+                    cols = slice(h * N_HALF, (h + 1) * N_HALF)
+                    acc = opsum.tile([P, N_HALF], F32)
+                    nc.tensor.matmul_mx(
+                        out=acc[:],
+                        lhsT=g_codes[:, rows].bitcast(E5M2X4),
+                        lhsT_scale=g_scales[:, rows],
+                        rhs=w_codes[:, cols].bitcast(E4M3X4),
+                        rhs_scale=w_scales[:, cols],
+                        start=True,
+                        stop=True,
+                    )
+                    dst = o_sb[:, b * N + h * N_HALF : b * N + (h + 1) * N_HALF]
+                    if 2 * b + h in VECTOR_BANKS:
+                        nc.vector.tensor_copy(out=dst, in_=acc[:])
+                    else:
+                        nc.scalar.copy(out=dst, in_=acc[:])
+                step = GROUP // pieces
+                if (b + 1) % step == 0:
+                    lo = b + 1 - step
+                    nc.sync.dma_start(
+                        out=out_rows[:, (j * GROUP + lo) * N : (j * GROUP + b + 1) * N],
+                        in_=o_sb[:, lo * N : (b + 1) * N],
+                    )
+
+        grouped = transpose_group(0, True)
+        prepare_w(0)
+        quantised = quantise_group(grouped)
+        prepare_w(1)
+        for j in range(GROUPS):
+            if j + 1 < GROUPS:
+                grouped = transpose_group(j + 1, False)
+            multiply_group(j, quantised[0], quantised[1], 2 if j == 0 else 1)
+            if j + 1 < GROUPS:
+                quantised = quantise_group(grouped)

@@ -21,7 +21,6 @@ TILES = 32
 GROUP = 4
 GROUPS = TILES // GROUP
 LOAD_CHUNKS = (4, 4, 8, 16)
-VECTOR_BANKS = (2, 6)
 
 
 def tile_sparselayer_t_kernel(tc, x, weights, bias, mask, grad_out, out):
@@ -32,11 +31,16 @@ def tile_sparselayer_t_kernel(tc, x, weights, bias, mask, grad_out, out):
         outs = ctx.enter_context(tc.tile_pool(name="outs", bufs=GROUPS))
         tpsum = ctx.enter_context(tc.psum_pool(name="tpsum", bufs=2))
         opsum = ctx.enter_context(tc.psum_pool(name="opsum", bufs=6))
+        ctx.enter_context(tc.manual_schedule())
 
         w_raw = keep.tile([P, 4 * N], BF16)
         m_raw = keep.tile([P, 4 * N], BF16)
-        nc.sync.dma_start(out=w_raw[:], in_=weights.rearrange("(p t) n -> p (t n)", t=4))
-        nc.sync.dma_start(out=m_raw[:], in_=mask.rearrange("(p t) n -> p (t n)", t=4))
+        w_rows = weights.rearrange("(p t) n -> p (t n)", t=4)
+        m_rows = mask.rearrange("(p t) n -> p (t n)", t=4)
+        for pair in range(2):
+            part = slice(pair * 2 * N, (pair + 1) * 2 * N)
+            nc.sync.dma_start(out=w_raw[:, part], in_=w_rows[:, part])
+            nc.sync.dma_start(out=m_raw[:, part], in_=m_rows[:, part])
         g_rows = grad_out.rearrange("(p i) k -> p (i k)", i=TILES)
         g_words = []
         first = 0
@@ -51,26 +55,41 @@ def tile_sparselayer_t_kernel(tc, x, weights, bias, mask, grad_out, out):
         ident = keep.tile([P, P], F32)
         make_identity(nc, ident[:])
 
+        w_masked = keep.tile([P, 4 * N], BF16)
         w_grouped = keep.tile([P, 4 * N], BF16, align_bytes=64)
         w_codes = keep.tile([P, N], U32, align_bytes=64)
         w_scales = keep.tile([P, N], U8, align_bytes=64)
 
-        def prepare_w(h):
-            cols = slice(h * N_HALF, (h + 1) * N_HALF)
-            flat = slice(h * 4 * N_HALF, (h + 1) * 4 * N_HALF)
+        def mask_w(pair):
+            part = slice(pair * 2 * N, (pair + 1) * 2 * N)
             nc.vector.tensor_tensor(
-                out=w_grouped[:, flat].rearrange("p (n t) -> p n t", t=4),
-                in0=w_raw[:].rearrange("p (t n) -> p t n", t=4)[:, :, cols].rearrange("p t n -> p n t"),
-                in1=m_raw[:].rearrange("p (t n) -> p t n", t=4)[:, :, cols].rearrange("p t n -> p n t"),
-                op=mybir.AluOpType.mult,
+                out=w_masked[:, part], in0=w_raw[:, part], in1=m_raw[:, part], op=mybir.AluOpType.mult
             )
+
+        def regroup_w(h):
+            src = w_masked[:].rearrange("p (t n) -> p t n", t=4)[:, :, h * N_HALF : (h + 1) * N_HALF]
+            nc.vector.tensor_copy(
+                out=w_grouped[:, h * 4 * N_HALF : (h + 1) * 4 * N_HALF].rearrange(
+                    "p (c i t) -> p c t i", i=4, t=4
+                ),
+                in_=src.rearrange("p t (c i) -> p c t i", i=4),
+            )
+
+        def quantise_w(h):
+            cols = slice(h * N_HALF, (h + 1) * N_HALF)
             nc.vector.quantize_mx(
                 out=w_codes[:, cols].bitcast(E4M3X4),
                 scales=w_scales[:, cols],
-                in_=w_grouped[:, flat],
+                in_=w_grouped[:, h * 4 * N_HALF : (h + 1) * 4 * N_HALF],
             )
 
-        def transpose_group(j, on_scalar):
+        def copy_out(on_vector, dst, src):
+            if on_vector:
+                nc.vector.tensor_copy(out=dst, in_=src)
+            else:
+                nc.scalar.copy(out=dst, in_=src)
+
+        def transpose_group(j, on_vector):
             g_grouped = stage.tile([P, GROUP * P * 4], BF16, align_bytes=64)
             g_grouped32 = g_grouped[:].bitcast(F32)
             for bank in range(GROUP // 2):
@@ -79,14 +98,11 @@ def tile_sparselayer_t_kernel(tc, x, weights, bias, mask, grad_out, out):
                     words = g_words[j * GROUP + 2 * bank + b].rearrange("p (w u) -> p u w", u=2)
                     for u in range(2):
                         nc.tensor.transpose(xt[:, b, u, :], words[:, u, :], ident[:])
-                dst = g_grouped32[:, bank * 512 : (bank + 1) * 512].rearrange(
-                    "p (b r u) -> p b r u", b=2, u=2
+                copy_out(
+                    on_vector,
+                    g_grouped32[:, bank * 512 : (bank + 1) * 512].rearrange("p (b r u) -> p b r u", b=2, u=2),
+                    xt[:].rearrange("p b u r -> p b r u"),
                 )
-                src = xt[:].rearrange("p b u r -> p b r u")
-                if on_scalar:
-                    nc.scalar.copy(out=dst, in_=src)
-                else:
-                    nc.vector.tensor_copy(out=dst, in_=src)
             return g_grouped
 
         def quantise_group(g_grouped):
@@ -95,44 +111,58 @@ def tile_sparselayer_t_kernel(tc, x, weights, bias, mask, grad_out, out):
             nc.vector.quantize_mx(out=g_codes[:].bitcast(E5M2X4), scales=g_scales[:], in_=g_grouped[:])
             return g_codes, g_scales
 
-        out_rows = out.rearrange("(p i) n -> p (i n)", i=TILES)
+        out_tiles = out.rearrange("(p i) n -> p i n", i=TILES)
 
-        def multiply_group(j, g_codes, g_scales, pieces):
-            o_sb = outs.tile([P, GROUP * N], F32)
-            for b in range(GROUP):
-                rows = slice(b * P, (b + 1) * P)
-                for h in range(2):
-                    cols = slice(h * N_HALF, (h + 1) * N_HALF)
-                    acc = opsum.tile([P, N_HALF], F32)
-                    nc.tensor.matmul_mx(
-                        out=acc[:],
-                        lhsT=g_codes[:, rows].bitcast(E5M2X4),
-                        lhsT_scale=g_scales[:, rows],
-                        rhs=w_codes[:, cols].bitcast(E4M3X4),
-                        rhs_scale=w_scales[:, cols],
-                        start=True,
-                        stop=True,
-                    )
-                    dst = o_sb[:, b * N + h * N_HALF : b * N + (h + 1) * N_HALF]
-                    if 2 * b + h in VECTOR_BANKS:
-                        nc.vector.tensor_copy(out=dst, in_=acc[:])
-                    else:
-                        nc.scalar.copy(out=dst, in_=acc[:])
-                step = GROUP // pieces
-                if (b + 1) % step == 0:
-                    lo = b + 1 - step
-                    nc.sync.dma_start(
-                        out=out_rows[:, (j * GROUP + lo) * N : (j * GROUP + b + 1) * N],
-                        in_=o_sb[:, lo * N : (b + 1) * N],
-                    )
+        def multiply(quantised, o_sb, b, h, on_vector):
+            rows = slice(b * P, (b + 1) * P)
+            cols = slice(h * N_HALF, (h + 1) * N_HALF)
+            acc = opsum.tile([P, N_HALF], F32)
+            nc.tensor.matmul_mx(
+                out=acc[:],
+                lhsT=quantised[0][:, rows].bitcast(E5M2X4),
+                lhsT_scale=quantised[1][:, rows],
+                rhs=w_codes[:, cols].bitcast(E4M3X4),
+                rhs_scale=w_scales[:, cols],
+                start=True,
+                stop=True,
+            )
+            copy_out(on_vector, o_sb[:, b, cols], acc[:])
 
-        grouped = transpose_group(0, True)
-        prepare_w(0)
+        def store(j, o_sb, b0, b1, c0, c1):
+            nc.sync.dma_start(out=out_tiles[:, j * GROUP + b0 : j * GROUP + b1, c0:c1], in_=o_sb[:, b0:b1, c0:c1])
+
+        mask_w(0)
+        mask_w(1)
+        regroup_w(0)
+        quantise_w(0)
+        grouped = transpose_group(0, False)
         quantised = quantise_group(grouped)
-        prepare_w(1)
-        for j in range(GROUPS):
+        regroup_w(1)
+        grouped = transpose_group(1, False)
+        o_sb = outs.tile([P, GROUP, N], F32)
+        for b in range(GROUP):
+            multiply(quantised, o_sb, b, 0, False)
+            if b % 2 == 1:
+                store(0, o_sb, b - 1, b + 1, 0, N_HALF)
+        quantise_w(1)
+        quantised_next = quantise_group(grouped)
+        for b in range(GROUP):
+            multiply(quantised, o_sb, b, 1, b % 2 == 1)
+            if b % 2 == 1:
+                store(0, o_sb, b - 1, b + 1, N_HALF, N)
+
+        banks = 0
+        for j in range(1, GROUPS):
+            quantised = quantised_next
             if j + 1 < GROUPS:
-                grouped = transpose_group(j + 1, False)
-            multiply_group(j, quantised[0], quantised[1], 2 if j == 0 else 1)
+                grouped = transpose_group(j + 1, True)
+            o_sb = outs.tile([P, GROUP, N], F32)
+            for b in range(GROUP):
+                for h in range(2):
+                    multiply(quantised, o_sb, b, h, banks % 3 == 2)
+                    banks += 1
+                if j == 1 and b == 1:
+                    store(j, o_sb, 0, 2, 0, N)
+            store(j, o_sb, 2 if j == 1 else 0, GROUP, 0, N)
             if j + 1 < GROUPS:
-                quantised = quantise_group(grouped)
+                quantised_next = quantise_group(grouped)

@@ -21,6 +21,7 @@ TILES = 32
 GROUP = 4
 GROUPS = TILES // GROUP
 LOAD_CHUNKS = (4, 4, 8, 16)
+DMA_ALIGN = 256
 
 
 def tile_sparselayer_t_kernel(tc, x, weights, bias, mask, grad_out, out):
@@ -33,8 +34,8 @@ def tile_sparselayer_t_kernel(tc, x, weights, bias, mask, grad_out, out):
         opsum = ctx.enter_context(tc.psum_pool(name="opsum", bufs=6))
         ctx.enter_context(tc.manual_schedule())
 
-        w_raw = keep.tile([P, 4 * N], BF16)
-        m_raw = keep.tile([P, 4 * N], BF16)
+        w_raw = keep.tile([P, 4 * N], BF16, align_bytes=DMA_ALIGN)
+        m_raw = keep.tile([P, 4 * N], BF16, align_bytes=DMA_ALIGN)
         w_rows = weights.rearrange("(p t) n -> p (t n)", t=4)
         m_rows = mask.rearrange("(p t) n -> p (t n)", t=4)
         for pair in range(2):
@@ -45,7 +46,7 @@ def tile_sparselayer_t_kernel(tc, x, weights, bias, mask, grad_out, out):
         g_words = []
         first = 0
         for c, count in enumerate(LOAD_CHUNKS):
-            g_raw = keep.tile([P, count * K], BF16, name="g_raw%d" % c)
+            g_raw = keep.tile([P, count * K], BF16, name="g_raw%d" % c, align_bytes=DMA_ALIGN)
             nc.sync.dma_start(out=g_raw[:], in_=g_rows[:, first * K : (first + count) * K])
             g32 = g_raw[:].bitcast(F32)
             for i in range(count):
@@ -139,7 +140,7 @@ def tile_sparselayer_t_kernel(tc, x, weights, bias, mask, grad_out, out):
         quantised = quantise_group(grouped)
         regroup_w(1)
         grouped = transpose_group(1, False)
-        o_sb = outs.tile([P, GROUP, N], F32)
+        o_sb = outs.tile([P, GROUP, N], F32, align_bytes=DMA_ALIGN)
         for b in range(GROUP):
             multiply(quantised, o_sb, b, 0, False)
             if b % 2 == 1:
@@ -156,7 +157,7 @@ def tile_sparselayer_t_kernel(tc, x, weights, bias, mask, grad_out, out):
             quantised = quantised_next
             if j + 1 < GROUPS:
                 grouped = transpose_group(j + 1, True)
-            o_sb = outs.tile([P, GROUP, N], F32)
+            o_sb = outs.tile([P, GROUP, N], F32, align_bytes=DMA_ALIGN)
             for b in range(GROUP):
                 for h in range(2):
                     multiply(quantised, o_sb, b, h, banks % 3 == 2)

@@ -38,9 +38,9 @@ def tile_sparselayer_t_kernel(tc, x, weights, bias, mask, grad_out, out):
         m_raw = keep.tile([P, 4 * N], BF16, align_bytes=DMA_ALIGN)
         w_rows = weights.rearrange("(p t) n -> p (t n)", t=4)
         m_rows = mask.rearrange("(p t) n -> p (t n)", t=4)
+        nc.sync.dma_start(out=w_raw[:], in_=w_rows)
         for pair in range(2):
             part = slice(pair * 2 * N, (pair + 1) * 2 * N)
-            nc.sync.dma_start(out=w_raw[:, part], in_=w_rows[:, part])
             nc.sync.dma_start(out=m_raw[:, part], in_=m_rows[:, part])
         g_rows = grad_out.rearrange("(p i) k -> p (i k)", i=TILES)
         g_words = []
@@ -162,8 +162,8 @@ def tile_sparselayer_t_kernel(tc, x, weights, bias, mask, grad_out, out):
                 for h in range(2):
                     multiply(quantised, o_sb, b, h, banks % 3 == 2)
                     banks += 1
-                if j == 1 and b == 1:
+                if j <= 2 and b == 1:
                     store(j, o_sb, 0, 2, 0, N)
-            store(j, o_sb, 2 if j == 1 else 0, GROUP, 0, N)
+            store(j, o_sb, 2 if j <= 2 else 0, GROUP, 0, N)
             if j + 1 < GROUPS:
                 quantised_next = quantise_group(grouped)

@@ -160,7 +160,7 @@ def tile_sparselayer_t_kernel(tc, x, weights, bias, mask, grad_out, out):
             o_sb = outs.tile([P, GROUP, N], F32, align_bytes=DMA_ALIGN)
             for b in range(GROUP):
                 for h in range(2):
-                    multiply(quantised, o_sb, b, h, banks % 3 == 2)
+                    multiply(quantised, o_sb, b, h, (j < 6 and 2 * b + h == 5) if j >= 4 else banks % 3 == 2)
                     banks += 1
                 if j <= 2 and b == 1:
                     store(j, o_sb, 0, 2, 0, N)

@@ -21,6 +21,7 @@ TILES = 32
 GROUP = 4
 GROUPS = TILES // GROUP
 LOAD_CHUNKS = (4, 4, 8, 16)
+HOLD = 32
 DMA_ALIGN = 256
 
 
@@ -45,13 +46,24 @@ def tile_sparselayer_t_kernel(tc, x, weights, bias, mask, grad_out, out):
         g_rows = grad_out.rearrange("(p i) k -> p (i k)", i=TILES)
         g_words = []
         first = 0
+        loads = []
         for c, count in enumerate(LOAD_CHUNKS):
             g_raw = keep.tile([P, count * K], BF16, name="g_raw%d" % c, align_bytes=DMA_ALIGN)
-            nc.sync.dma_start(out=g_raw[:], in_=g_rows[:, first * K : (first + count) * K])
+            loads.append((g_raw, g_rows[:, first * K : (first + count) * K]))
             g32 = g_raw[:].bitcast(F32)
             for i in range(count):
                 g_words.append(g32[:, i * (K // 2) : (i + 1) * (K // 2)])
             first += count
+
+        def load_g(c):
+            nc.sync.dma_start(out=loads[c][0][:], in_=loads[c][1])
+
+        load_g(0)
+        load_g(1)
+        nc.scalar.copy(out=loads[2][0][:, :HOLD], in_=w_raw[:, :HOLD])
+        load_g(2)
+        nc.scalar.copy(out=loads[3][0][:, :HOLD], in_=m_raw[:, :HOLD])
+        load_g(3)
 
         ident = keep.tile([P, P], F32)
         make_identity(nc, ident[:])

from contextlib import ExitStack

import concourse.mybir as mybir
from concourse.masks import make_identity

FLOPS = 2 * 4096 * 512 * 1024
BYTES = 4096 * 1024 * 4 + 4096 * 512 * 2 + 2 * 512 * 1024 * 2

F32 = mybir.dt.float32
BF16 = mybir.dt.bfloat16
U32 = mybir.dt.uint32
U8 = mybir.dt.uint8
E4M3X4 = mybir.dt.float8_e4m3fn_x4
E5M2X4 = mybir.dt.float8_e5m2_x4

P = 128
K = 512
N = 1024
N_HALF = 512
TILES = 32
GROUP = 4
GROUPS = TILES // GROUP
LOAD_CHUNKS = (4, 4, 8, 16)
HOLD = 32
DMA_ALIGN = 256


def tile_sparselayer_t_kernel(tc, x, weights, bias, mask, grad_out, out):
    nc = tc.nc
    with ExitStack() as ctx:
        keep = ctx.enter_context(tc.tile_pool(name="keep", bufs=1))
        stage = ctx.enter_context(tc.tile_pool(name="stage", bufs=3))
        outs = ctx.enter_context(tc.tile_pool(name="outs", bufs=GROUPS))
        tpsum = ctx.enter_context(tc.psum_pool(name="tpsum", bufs=2))
        opsum = ctx.enter_context(tc.psum_pool(name="opsum", bufs=6))
        ctx.enter_context(tc.manual_schedule())

        w_raw = keep.tile([P, 4 * N], BF16, align_bytes=DMA_ALIGN)
        m_raw = keep.tile([P, 4 * N], BF16, align_bytes=DMA_ALIGN)
        w_rows = weights.rearrange("(p t) n -> p (t n)", t=4)
        m_rows = mask.rearrange("(p t) n -> p (t n)", t=4)
        nc.sync.dma_start(out=w_raw[:], in_=w_rows)
        for pair in range(2):
            part = slice(pair * 2 * N, (pair + 1) * 2 * N)
            nc.sync.dma_start(out=m_raw[:, part], in_=m_rows[:, part])
        g_rows = grad_out.rearrange("(p i) k -> p (i k)", i=TILES)
        g_words = []
        first = 0
        loads = []
        for c, count in enumerate(LOAD_CHUNKS):
            g_raw = keep.tile([P, count * K], BF16, name="g_raw%d" % c, align_bytes=DMA_ALIGN)
            loads.append((g_raw, g_rows[:, first * K : (first + count) * K]))
            g32 = g_raw[:].bitcast(F32)
            for i in range(count):
                g_words.append(g32[:, i * (K // 2) : (i + 1) * (K // 2)])
            first += count

        def load_g(c):
            nc.sync.dma_start(out=loads[c][0][:], in_=loads[c][1])

        load_g(0)
        load_g(1)
        nc.scalar.copy(out=loads[2][0][:, :HOLD], in_=w_raw[:, :HOLD])
        load_g(2)
        nc.scalar.copy(out=loads[3][0][:, :HOLD], in_=m_raw[:, :HOLD])
        load_g(3)

        ident = keep.tile([P, P], F32)
        make_identity(nc, ident[:])

        w_masked = keep.tile([P, 4 * N], BF16)
        w_grouped = keep.tile([P, 4 * N], BF16, align_bytes=64)
        w_codes = keep.tile([P, N], U32, align_bytes=64)
        w_scales = keep.tile([P, N], U8, align_bytes=64)

        def mask_w(pair):
            part = slice(pair * 2 * N, (pair + 1) * 2 * N)
            nc.vector.tensor_tensor(
                out=w_masked[:, part], in0=w_raw[:, part], in1=m_raw[:, part], op=mybir.AluOpType.mult
            )

        def regroup_w(h):
            src = w_masked[:].rearrange("p (t n) -> p t n", t=4)[:, :, h * N_HALF : (h + 1) * N_HALF]
            nc.vector.tensor_copy(
                out=w_grouped[:, h * 4 * N_HALF : (h + 1) * 4 * N_HALF].rearrange(
                    "p (c i t) -> p c t i", i=4, t=4
                ),
                in_=src.rearrange("p t (c i) -> p c t i", i=4),
            )

        def quantise_w(h):
            cols = slice(h * N_HALF, (h + 1) * N_HALF)
            nc.vector.quantize_mx(
                out=w_codes[:, cols].bitcast(E4M3X4),
                scales=w_scales[:, cols],
                in_=w_grouped[:, h * 4 * N_HALF : (h + 1) * 4 * N_HALF],
            )

        def copy_out(on_vector, dst, src):
            if on_vector:
                nc.vector.tensor_copy(out=dst, in_=src)
            else:
                nc.scalar.copy(out=dst, in_=src)

        def transpose_group(j, on_vector):
            g_grouped = stage.tile([P, GROUP * P * 4], BF16, align_bytes=64)
            g_grouped32 = g_grouped[:].bitcast(F32)
            for bank in range(GROUP // 2):
                xt = tpsum.tile([P, 2, 2, P], F32)
                for b in range(2):
                    words = g_words[j * GROUP + 2 * bank + b].rearrange("p (w u) -> p u w", u=2)
                    for u in range(2):
                        nc.tensor.transpose(xt[:, b, u, :], words[:, u, :], ident[:])
                copy_out(
                    on_vector,
                    g_grouped32[:, bank * 512 : (bank + 1) * 512].rearrange("p (b r u) -> p b r u", b=2, u=2),
                    xt[:].rearrange("p b u r -> p b r u"),
                )
            return g_grouped

        def quantise_group(g_grouped):
            g_codes = stage.tile([P, GROUP * P], U32, align_bytes=64)
            g_scales = stage.tile([P, GROUP * P], U8, align_bytes=64)
            nc.vector.quantize_mx(out=g_codes[:].bitcast(E5M2X4), scales=g_scales[:], in_=g_grouped[:])
            return g_codes, g_scales

        out_tiles = out.rearrange("(p i) n -> p i n", i=TILES)

        def multiply(quantised, o_sb, b, h, on_vector):
            rows = slice(b * P, (b + 1) * P)
            cols = slice(h * N_HALF, (h + 1) * N_HALF)
            acc = opsum.tile([P, N_HALF], F32)
            nc.tensor.matmul_mx(
                out=acc[:],
                lhsT=quantised[0][:, rows].bitcast(E5M2X4),
                lhsT_scale=quantised[1][:, rows],
                rhs=w_codes[:, cols].bitcast(E4M3X4),
                rhs_scale=w_scales[:, cols],
                start=True,
                stop=True,
            )
            copy_out(on_vector, o_sb[:, b, cols], acc[:])

        def store(j, o_sb, b0, b1, c0, c1):
            nc.sync.dma_start(out=out_tiles[:, j * GROUP + b0 : j * GROUP + b1, c0:c1], in_=o_sb[:, b0:b1, c0:c1])

        mask_w(0)
        mask_w(1)
        regroup_w(0)
        quantise_w(0)
        grouped = transpose_group(0, False)
        quantised = quantise_group(grouped)
        regroup_w(1)
        grouped = transpose_group(1, False)
        o_sb = outs.tile([P, GROUP, N], F32, align_bytes=DMA_ALIGN)
        for b in range(GROUP):
            multiply(quantised, o_sb, b, 0, False)
            if b % 2 == 1:
                store(0, o_sb, b - 1, b + 1, 0, N_HALF)
        quantise_w(1)
        quantised_next = quantise_group(grouped)
        for b in range(GROUP):
            multiply(quantised, o_sb, b, 1, b % 2 == 1)
            if b % 2 == 1:
                store(0, o_sb, b - 1, b + 1, N_HALF, N)

        banks = 0
        for j in range(1, GROUPS):
            quantised = quantised_next
            if j + 1 < GROUPS:
                grouped = transpose_group(j + 1, True)
            o_sb = outs.tile([P, GROUP, N], F32, align_bytes=DMA_ALIGN)
            for b in range(GROUP):
                for h in range(2):
                    multiply(quantised, o_sb, b, h, (j < 6 and 2 * b + h == 5) if j >= 4 else banks % 3 == 2)
                    banks += 1
                if j <= 2 and b == 1:
                    store(j, o_sb, 0, 2, 0, N)
            store(j, o_sb, 2 if j <= 2 else 0, GROUP, 0, N)
            if j + 1 < GROUPS:
                quantised_next = quantise_group(grouped)
